import numpy as np
import ml_dtypes

BF16 = ml_dtypes.bfloat16


def bf(x):
    return np.asarray(x, np.float32).astype(BF16)


def f32(x):
    return np.asarray(x, np.float32)


def f64(x):
    return np.asarray(x).astype(np.float64)


def striped(idx):
    return np.tile(idx.reshape(-1, 16).T, (8, 1))


C, S, H, K, N = 256, 256, 128, 8, 1024
EPS = 1.0


def setup_inputs():
    return {"learnable_mask": f32(np.random.uniform(-2.0, 2.0, (C, S))), "offs": striped(np.concatenate([np.random.permutation(S)[:H] for _ in range(K)]))}


def reference(learnable_mask, offs):
    idx = offs[:16].T.reshape(-1)
    m01 = np.where(np.abs(f64(learnable_mask)) > EPS, 1.0, 0.0)
    return m01[:, idx]

@@ -1,0 +1,43 @@
+import concourse.mybir as mybir
+
+F32 = mybir.dt.float32
+U16 = mybir.dt.uint16
+MULT = mybir.AluOpType.mult
+IS_GT = mybir.AluOpType.is_gt
+COPY = mybir.ActivationFunctionType.Copy
+
+P = 128
+FEATURES = 256
+FORMULAS = 256
+LITERALS = 1024
+PER_COLUMN = 16
+PIECE = FORMULAS
+
+
+def tile_featureselection_kernel(tc, learnable_mask, offs, out):
+    nc = tc.nc
+    with (
+        tc.tile_pool(name="held", bufs=1) as held,
+        tc.tile_pool(name="windows", bufs=2) as windows,
+        tc.tile_pool(name="expanded", bufs=4) as expanded,
+    ):
+        offsets = held.tile([P, LITERALS // PER_COLUMN], U16, name="offsets")
+        nc.sync.dma_start(offsets[:], offs)
+
+        for block in range(FEATURES // P):
+            rows = slice(block * P, (block + 1) * P)
+
+            raw = windows.tile([P, FORMULAS], F32)
+            nc.scalar.dma_start(raw[:], learnable_mask[rows, :])
+
+            squared = windows.tile([P, FORMULAS], F32)
+            nc.vector.tensor_tensor(squared[:], raw[:], raw[:], MULT)
+            m01 = windows.tile([P, FORMULAS], F32)
+            nc.vector.tensor_scalar(m01[:], squared[:], 1.0, None, IS_GT)
+
+            for piece in range(LITERALS // PIECE):
+                columns = slice(piece * PIECE, (piece + 1) * PIECE)
+                part = slice(piece * PIECE // PER_COLUMN, (piece + 1) * PIECE // PER_COLUMN)
+                literals = expanded.tile([P, PIECE], F32)
+                nc.scalar.activation(literals[:], m01[:].indirect(offsets[:, part]), COPY)
+                nc.sync.dma_start(out[rows, columns], literals[:])

@@ -19,7 +19,7 @@ def tile_featureselection_kernel(tc, learnable_mask, offs, out):
     with (
         tc.tile_pool(name="held", bufs=1) as held,
         tc.tile_pool(name="windows", bufs=2) as windows,
-        tc.tile_pool(name="expanded", bufs=4) as expanded,
+        tc.tile_pool(name="expanded", bufs=2) as expanded,
     ):
         offsets = held.tile([P, LITERALS // PER_COLUMN], U16, name="offsets")
         nc.sync.dma_start(offsets[:], offs)
@@ -35,9 +35,9 @@ def tile_featureselection_kernel(tc, learnable_mask, offs, out):
             m01 = windows.tile([P, FORMULAS], F32)
             nc.vector.tensor_scalar(m01[:], squared[:], 1.0, None, IS_GT)
 
+            literals = expanded.tile([P, LITERALS], F32)
             for piece in range(LITERALS // PIECE):
                 columns = slice(piece * PIECE, (piece + 1) * PIECE)
                 part = slice(piece * PIECE // PER_COLUMN, (piece + 1) * PIECE // PER_COLUMN)
-                literals = expanded.tile([P, PIECE], F32)
-                nc.scalar.activation(literals[:], m01[:].indirect(offsets[:, part]), COPY)
-                nc.sync.dma_start(out[rows, columns], literals[:])
+                nc.scalar.activation(literals[:, columns], m01[:].indirect(offsets[:, part]), COPY)
+                nc.sync.dma_start(out[rows, columns], literals[:, columns])

@@ -11,6 +11,7 @@ FEATURES = 256
 FORMULAS = 256
 LITERALS = 1024
 PER_COLUMN = 16
+BLOCKS = FEATURES // P
 PIECE = FORMULAS
 
 
@@ -21,17 +22,18 @@ def tile_featureselection_kernel(tc, learnable_mask, offs, out):
         tc.tile_pool(name="windows", bufs=2) as windows,
         tc.tile_pool(name="expanded", bufs=2) as expanded,
     ):
+        raw = [held.tile([P, FORMULAS], F32, name=f"raw{block}") for block in range(BLOCKS)]
         offsets = held.tile([P, LITERALS // PER_COLUMN], U16, name="offsets")
-        nc.sync.dma_start(offsets[:], offs)
 
-        for block in range(FEATURES // P):
+        nc.sync.dma_start(raw[0][:], learnable_mask[0:P, :])
+        nc.sync.dma_start(offsets[:], offs)
+        nc.sync.dma_start(raw[1][:], learnable_mask[P : 2 * P, :])
+
+        for block in range(BLOCKS):
             rows = slice(block * P, (block + 1) * P)
 
-            raw = windows.tile([P, FORMULAS], F32)
-            nc.scalar.dma_start(raw[:], learnable_mask[rows, :])
-
             squared = windows.tile([P, FORMULAS], F32)
-            nc.vector.tensor_tensor(squared[:], raw[:], raw[:], MULT)
+            nc.vector.tensor_tensor(squared[:], raw[block][:], raw[block][:], MULT)
             m01 = windows.tile([P, FORMULAS], F32)
             nc.vector.tensor_scalar(m01[:], squared[:], 1.0, None, IS_GT)
 

@@ -29,6 +29,10 @@ def tile_featureselection_kernel(tc, learnable_mask, offs, out):
         nc.sync.dma_start(offsets[:], offs)
         nc.sync.dma_start(raw[1][:], learnable_mask[P : 2 * P, :])
 
+        warm = held.tile([P, 1], F32, name="warm")
+        nc.gpsimd.memset(warm[:], 0.0)
+        nc.scalar.activation(warm[:], warm[:], COPY)
+
         for block in range(BLOCKS):
             rows = slice(block * P, (block + 1) * P)
 

@@ -2,7 +2,8 @@ import concourse.mybir as mybir
 
 F32 = mybir.dt.float32
 U16 = mybir.dt.uint16
-MULT = mybir.AluOpType.mult
+I32 = mybir.dt.int32
+AND = mybir.AluOpType.bitwise_and
 IS_GT = mybir.AluOpType.is_gt
 COPY = mybir.ActivationFunctionType.Copy
 
@@ -12,6 +13,7 @@ FORMULAS = 256
 LITERALS = 1024
 PER_COLUMN = 16
 BLOCKS = FEATURES // P
+SIGN_CLEARED = 0x7FFFFFFF
 PIECE = FORMULAS
 
 
@@ -36,10 +38,12 @@ def tile_featureselection_kernel(tc, learnable_mask, offs, out):
         for block in range(BLOCKS):
             rows = slice(block * P, (block + 1) * P)
 
-            squared = windows.tile([P, FORMULAS], F32)
-            nc.vector.tensor_tensor(squared[:], raw[block][:], raw[block][:], MULT)
+            magnitude = windows.tile([P, FORMULAS], F32)
+            nc.vector.tensor_scalar(
+                magnitude[:].bitcast(I32), raw[block][:].bitcast(I32), SIGN_CLEARED, None, AND
+            )
             m01 = windows.tile([P, FORMULAS], F32)
-            nc.vector.tensor_scalar(m01[:], squared[:], 1.0, None, IS_GT)
+            nc.vector.tensor_scalar(m01[:], magnitude[:], 1.0, None, IS_GT)
 
             literals = expanded.tile([P, LITERALS], F32)
             for piece in range(LITERALS // PIECE):

@@ -15,6 +15,7 @@ PER_COLUMN = 16
 BLOCKS = FEATURES // P
 SIGN_CLEARED = 0x7FFFFFFF
 PIECE = FORMULAS
+LAST_PIECE = 64
 
 
 def tile_featureselection_kernel(tc, learnable_mask, offs, out):
@@ -45,9 +46,13 @@ def tile_featureselection_kernel(tc, learnable_mask, offs, out):
             m01 = windows.tile([P, FORMULAS], F32)
             nc.vector.tensor_scalar(m01[:], magnitude[:], 1.0, None, IS_GT)
 
+            edges = list(range(0, LITERALS, PIECE)) + [LITERALS]
+            if block == BLOCKS - 1:
+                edges = edges[:-1] + [LITERALS - LAST_PIECE, LITERALS]
             literals = expanded.tile([P, LITERALS], F32)
-            for piece in range(LITERALS // PIECE):
-                columns = slice(piece * PIECE, (piece + 1) * PIECE)
-                part = slice(piece * PIECE // PER_COLUMN, (piece + 1) * PIECE // PER_COLUMN)
-                nc.scalar.activation(literals[:, columns], m01[:].indirect(offsets[:, part]), COPY)
-                nc.sync.dma_start(out[rows, columns], literals[:, columns])
+            for first, end in zip(edges[:-1], edges[1:]):
+                part = slice(first // PER_COLUMN, end // PER_COLUMN)
+                nc.scalar.activation(
+                    literals[:, first:end], m01[:].indirect(offsets[:, part]), COPY
+                )
+                nc.sync.dma_start(out[rows, first:end], literals[:, first:end])

@@ -33,7 +33,7 @@ def tile_featureselection_kernel(tc, learnable_mask, offs, out):
         nc.sync.dma_start(raw[1][:], learnable_mask[P : 2 * P, :])
 
         warm = held.tile([P, 1], F32, name="warm")
-        nc.gpsimd.memset(warm[:], 0.0)
+        nc.vector.memset(warm[:], 0.0)
         nc.scalar.activation(warm[:], warm[:], COPY)
 
         for block in range(BLOCKS):

@@ -15,7 +15,7 @@ PER_COLUMN = 16
 BLOCKS = FEATURES // P
 SIGN_CLEARED = 0x7FFFFFFF
 PIECE = FORMULAS
-LAST_PIECE = 64
+LAST_PIECE = 128
 
 
 def tile_featureselection_kernel(tc, learnable_mask, offs, out):

@@ -40,11 +40,18 @@ def tile_featureselection_kernel(tc, learnable_mask, offs, out):
             rows = slice(block * P, (block + 1) * P)
 
             magnitude = windows.tile([P, FORMULAS], F32)
-            nc.vector.tensor_scalar(
-                magnitude[:].bitcast(I32), raw[block][:].bitcast(I32), SIGN_CLEARED, None, AND
-            )
             m01 = windows.tile([P, FORMULAS], F32)
-            nc.vector.tensor_scalar(m01[:], magnitude[:], 1.0, None, IS_GT)
+            halves = [slice(0, FORMULAS // 2), slice(FORMULAS // 2, FORMULAS)]
+            for half in halves:
+                nc.vector.tensor_scalar(
+                    magnitude[:, half].bitcast(I32),
+                    raw[block][:, half].bitcast(I32),
+                    SIGN_CLEARED,
+                    None,
+                    AND,
+                )
+            for half in halves:
+                nc.vector.tensor_scalar(m01[:, half], magnitude[:, half], 1.0, None, IS_GT)
 
             edges = list(range(0, LITERALS, PIECE)) + [LITERALS]
             if block == BLOCKS - 1:

@@ -62,4 +62,7 @@ def tile_featureselection_kernel(tc, learnable_mask, offs, out):
                 nc.scalar.activation(
                     literals[:, first:end], m01[:].indirect(offsets[:, part]), COPY
                 )
-                nc.sync.dma_start(out[rows, first:end], literals[:, first:end])
+                step = (end - first) // 2 if block == 0 else end - first
+                for column in range(first, end, step):
+                    piece = slice(column, column + step)
+                    nc.sync.dma_start(out[rows, piece], literals[:, piece])

@@ -57,12 +57,17 @@ def tile_featureselection_kernel(tc, learnable_mask, offs, out):
             if block == BLOCKS - 1:
                 edges = edges[:-1] + [LITERALS - LAST_PIECE, LITERALS]
             literals = expanded.tile([P, LITERALS], F32)
+            stored = 0
+            store_ends = [LITERALS]
+            if block == BLOCKS - 1:
+                store_ends = [LITERALS - 4 * LAST_PIECE]
+                store_ends += [LITERALS - 2 * LAST_PIECE, LITERALS - LAST_PIECE, LITERALS]
             for first, end in zip(edges[:-1], edges[1:]):
                 part = slice(first // PER_COLUMN, end // PER_COLUMN)
                 nc.scalar.activation(
                     literals[:, first:end], m01[:].indirect(offsets[:, part]), COPY
                 )
-                step = (end - first) // 2 if block == 0 else end - first
-                for column in range(first, end, step):
-                    piece = slice(column, column + step)
+                if end in store_ends:
+                    piece = slice(stored, end)
                     nc.sync.dma_start(out[rows, piece], literals[:, piece])
+                    stored = end

@@ -22,6 +22,7 @@ def tile_featureselection_kernel(tc, learnable_mask, offs, out):
     nc = tc.nc
     with (
         tc.tile_pool(name="held", bufs=1) as held,
+        tc.tile_pool(name="magnitudes", bufs=1) as magnitudes,
         tc.tile_pool(name="windows", bufs=2) as windows,
         tc.tile_pool(name="expanded", bufs=2) as expanded,
     ):
@@ -30,16 +31,16 @@ def tile_featureselection_kernel(tc, learnable_mask, offs, out):
 
         nc.sync.dma_start(raw[0][:], learnable_mask[0:P, :])
         nc.sync.dma_start(offsets[:], offs)
-        nc.sync.dma_start(raw[1][:], learnable_mask[P : 2 * P, :])
 
-        warm = held.tile([P, 1], F32, name="warm")
-        nc.vector.memset(warm[:], 0.0)
-        nc.scalar.activation(warm[:], warm[:], COPY)
+        warm = raw[1][:, 0:1]
+        nc.vector.memset(warm, 0.0)
+        nc.scalar.activation(warm, warm, COPY)
+        nc.sync.dma_start(raw[1][:], learnable_mask[P : 2 * P, :])
 
         for block in range(BLOCKS):
             rows = slice(block * P, (block + 1) * P)
 
-            magnitude = windows.tile([P, FORMULAS], F32)
+            magnitude = magnitudes.tile([P, FORMULAS], F32)
             m01 = windows.tile([P, FORMULAS], F32)
             halves = [slice(0, FORMULAS // 2), slice(FORMULAS // 2, FORMULAS)]
             for half in halves:

@@ -26,20 +26,21 @@ def tile_featureselection_kernel(tc, learnable_mask, offs, out):
         tc.tile_pool(name="windows", bufs=2) as windows,
         tc.tile_pool(name="expanded", bufs=2) as expanded,
     ):
+        mask_blocks = learnable_mask.rearrange("(p b) f -> p b f", b=BLOCKS)
+        out_blocks = out.rearrange("(p b) j -> p b j", b=BLOCKS)
+
         raw = [held.tile([P, FORMULAS], F32, name=f"raw{block}") for block in range(BLOCKS)]
         offsets = held.tile([P, LITERALS // PER_COLUMN], U16, name="offsets")
 
-        nc.sync.dma_start(raw[0][:], learnable_mask[0:P, :])
+        nc.sync.dma_start(raw[0][:], mask_blocks[:, 0, :])
         nc.sync.dma_start(offsets[:], offs)
 
         warm = raw[1][:, 0:1]
         nc.vector.memset(warm, 0.0)
         nc.scalar.activation(warm, warm, COPY)
-        nc.sync.dma_start(raw[1][:], learnable_mask[P : 2 * P, :])
+        nc.sync.dma_start(raw[1][:], mask_blocks[:, 1, :])
 
         for block in range(BLOCKS):
-            rows = slice(block * P, (block + 1) * P)
-
             magnitude = magnitudes.tile([P, FORMULAS], F32)
             m01 = windows.tile([P, FORMULAS], F32)
             halves = [slice(0, FORMULAS // 2), slice(FORMULAS // 2, FORMULAS)]
@@ -70,5 +71,5 @@ def tile_featureselection_kernel(tc, learnable_mask, offs, out):
                 )
                 if end in store_ends:
                     piece = slice(stored, end)
-                    nc.sync.dma_start(out[rows, piece], literals[:, piece])
+                    nc.sync.dma_start(out_blocks[:, block, piece], literals[:, piece])
                     stored = end

@@ -13,6 +13,7 @@ FORMULAS = 256
 LITERALS = 1024
 PER_COLUMN = 16
 BLOCKS = FEATURES // P
+COLUMNS = BLOCKS * LITERALS
 SIGN_CLEARED = 0x7FFFFFFF
 PIECE = FORMULAS
 LAST_PIECE = 128
@@ -20,17 +21,18 @@ LAST_PIECE = 128
 
 def tile_featureselection_kernel(tc, learnable_mask, offs, out):
     nc = tc.nc
+
+    mask_blocks = learnable_mask.rearrange("(p b) f -> p b f", b=BLOCKS)
+    out_rows = out.rearrange("(p b) j -> p (b j)", b=BLOCKS)
+
     with (
         tc.tile_pool(name="held", bufs=1) as held,
         tc.tile_pool(name="magnitudes", bufs=1) as magnitudes,
-        tc.tile_pool(name="windows", bufs=2) as windows,
-        tc.tile_pool(name="expanded", bufs=2) as expanded,
+        tc.tile_pool(name="windows", bufs=BLOCKS) as windows,
     ):
-        mask_blocks = learnable_mask.rearrange("(p b) f -> p b f", b=BLOCKS)
-        out_blocks = out.rearrange("(p b) j -> p b j", b=BLOCKS)
-
         raw = [held.tile([P, FORMULAS], F32, name=f"raw{block}") for block in range(BLOCKS)]
         offsets = held.tile([P, LITERALS // PER_COLUMN], U16, name="offsets")
+        literals = held.tile([P, COLUMNS], F32, name="literals")
 
         nc.sync.dma_start(raw[0][:], mask_blocks[:, 0, :])
         nc.sync.dma_start(offsets[:], offs)
@@ -40,6 +42,7 @@ def tile_featureselection_kernel(tc, learnable_mask, offs, out):
         nc.scalar.activation(warm, warm, COPY)
         nc.sync.dma_start(raw[1][:], mask_blocks[:, 1, :])
 
+        stored = 0
         for block in range(BLOCKS):
             magnitude = magnitudes.tile([P, FORMULAS], F32)
             m01 = windows.tile([P, FORMULAS], F32)
@@ -58,18 +61,13 @@ def tile_featureselection_kernel(tc, learnable_mask, offs, out):
             edges = list(range(0, LITERALS, PIECE)) + [LITERALS]
             if block == BLOCKS - 1:
                 edges = edges[:-1] + [LITERALS - LAST_PIECE, LITERALS]
-            literals = expanded.tile([P, LITERALS], F32)
-            stored = 0
-            store_ends = [LITERALS]
-            if block == BLOCKS - 1:
-                store_ends = [LITERALS - 4 * LAST_PIECE]
-                store_ends += [LITERALS - 2 * LAST_PIECE, LITERALS - LAST_PIECE, LITERALS]
             for first, end in zip(edges[:-1], edges[1:]):
                 part = slice(first // PER_COLUMN, end // PER_COLUMN)
+                start, made = block * LITERALS + first, block * LITERALS + end
                 nc.scalar.activation(
-                    literals[:, first:end], m01[:].indirect(offsets[:, part]), COPY
+                    literals[:, start:made], m01[:].indirect(offsets[:, part]), COPY
                 )
-                if end in store_ends:
-                    piece = slice(stored, end)
-                    nc.sync.dma_start(out_blocks[:, block, piece], literals[:, piece])
-                    stored = end
+
+                if made - stored >= max((COLUMNS - stored) // 2, LAST_PIECE):
+                    nc.sync.dma_start(out_rows[:, stored:made], literals[:, stored:made])
+                    stored = made

@@ -46,17 +46,17 @@ def tile_featureselection_kernel(tc, learnable_mask, offs, out):
         for block in range(BLOCKS):
             magnitude = magnitudes.tile([P, FORMULAS], F32)
             m01 = windows.tile([P, FORMULAS], F32)
-            halves = [slice(0, FORMULAS // 2), slice(FORMULAS // 2, FORMULAS)]
-            for half in halves:
+            quarters = [slice(f, f + FORMULAS // 4) for f in range(0, FORMULAS, FORMULAS // 4)]
+            for quarter in quarters:
                 nc.vector.tensor_scalar(
-                    magnitude[:, half].bitcast(I32),
-                    raw[block][:, half].bitcast(I32),
+                    magnitude[:, quarter].bitcast(I32),
+                    raw[block][:, quarter].bitcast(I32),
                     SIGN_CLEARED,
                     None,
                     AND,
                 )
-            for half in halves:
-                nc.vector.tensor_scalar(m01[:, half], magnitude[:, half], 1.0, None, IS_GT)
+            for quarter in quarters:
+                nc.vector.tensor_scalar(m01[:, quarter], magnitude[:, quarter], 1.0, None, IS_GT)
 
             edges = list(range(0, LITERALS, PIECE)) + [LITERALS]
             if block == BLOCKS - 1:

import concourse.mybir as mybir

F32 = mybir.dt.float32
U16 = mybir.dt.uint16
I32 = mybir.dt.int32
AND = mybir.AluOpType.bitwise_and
IS_GT = mybir.AluOpType.is_gt
COPY = mybir.ActivationFunctionType.Copy

P = 128
FEATURES = 256
FORMULAS = 256
LITERALS = 1024
PER_COLUMN = 16
BLOCKS = FEATURES // P
COLUMNS = BLOCKS * LITERALS
SIGN_CLEARED = 0x7FFFFFFF
PIECE = FORMULAS
LAST_PIECE = 128


def tile_featureselection_kernel(tc, learnable_mask, offs, out):
    nc = tc.nc

    mask_blocks = learnable_mask.rearrange("(p b) f -> p b f", b=BLOCKS)
    out_rows = out.rearrange("(p b) j -> p (b j)", b=BLOCKS)

    with (
        tc.tile_pool(name="held", bufs=1) as held,
        tc.tile_pool(name="magnitudes", bufs=1) as magnitudes,
        tc.tile_pool(name="windows", bufs=BLOCKS) as windows,
    ):
        raw = [held.tile([P, FORMULAS], F32, name=f"raw{block}") for block in range(BLOCKS)]
        offsets = held.tile([P, LITERALS // PER_COLUMN], U16, name="offsets")
        literals = held.tile([P, COLUMNS], F32, name="literals")

        nc.sync.dma_start(raw[0][:], mask_blocks[:, 0, :])
        nc.sync.dma_start(offsets[:], offs)

        warm = raw[1][:, 0:1]
        nc.vector.memset(warm, 0.0)
        nc.scalar.activation(warm, warm, COPY)
        nc.sync.dma_start(raw[1][:], mask_blocks[:, 1, :])

        stored = 0
        for block in range(BLOCKS):
            magnitude = magnitudes.tile([P, FORMULAS], F32)
            m01 = windows.tile([P, FORMULAS], F32)
            quarters = [slice(f, f + FORMULAS // 4) for f in range(0, FORMULAS, FORMULAS // 4)]
            for quarter in quarters:
                nc.vector.tensor_scalar(
                    magnitude[:, quarter].bitcast(I32),
                    raw[block][:, quarter].bitcast(I32),
                    SIGN_CLEARED,
                    None,
                    AND,
                )
            for quarter in quarters:
                nc.vector.tensor_scalar(m01[:, quarter], magnitude[:, quarter], 1.0, None, IS_GT)

            edges = list(range(0, LITERALS, PIECE)) + [LITERALS]
            if block == BLOCKS - 1:
                edges = edges[:-1] + [LITERALS - LAST_PIECE, LITERALS]
            for first, end in zip(edges[:-1], edges[1:]):
                part = slice(first // PER_COLUMN, end // PER_COLUMN)
                start, made = block * LITERALS + first, block * LITERALS + end
                nc.scalar.activation(
                    literals[:, start:made], m01[:].indirect(offsets[:, part]), COPY
                )

                if made - stored >= max((COLUMNS - stored) // 2, LAST_PIECE):
                    nc.sync.dma_start(out_rows[:, stored:made], literals[:, stored:made])
                    stored = made
